import numpy as np
import ml_dtypes


def mxq(x, axis, fmt="e4m3"):
    dtype, down = {"e4m3": (ml_dtypes.float8_e4m3fn, 7), "e5m2": (ml_dtypes.float8_e5m2, 14)}[fmt]
    v = np.moveaxis(np.asarray(x, np.float32).astype(ml_dtypes.bfloat16).astype(np.float64), axis, -1)
    blocks = v.reshape(v.shape[:-1] + (-1, 32))
    amax = np.abs(blocks).max(-1, keepdims=True)
    byte = np.maximum(np.where(amax > 0, np.frexp(amax)[1] - 1 + 127, 0) - down, 1)
    scale = np.exp2(byte - 127.0)
    codes = (blocks / scale).astype(np.float32).astype(dtype).astype(np.float64)
    return np.moveaxis((codes * scale).reshape(v.shape), -1, axis)


WIDE = False


def mx_kscale(k):
    if not WIDE:
        return np.ones(k)
    levels = np.array([10, -10, 5, -5, 0])
    a = np.random.permutation(np.resize(levels, k // 512 * 4)).reshape(k // 512, 4)
    idx = np.arange(k)
    return np.exp2(a[idx // 512, idx % 128 // 32])


BF16 = ml_dtypes.bfloat16


def bf(x):
    return np.asarray(x, np.float32).astype(BF16)


def f64(x):
    return np.asarray(x).astype(np.float64)


E2M1 = np.array([0.0, 0.5, 1.0, 1.5, 2.0, 3.0, 4.0, 6.0, -0.0, -0.5, -1.0, -1.5, -2.0, -3.0, -4.0, -6.0])


def pack_weight(w, fmt):
    k, n = w.shape
    w = f64(bf(w)).reshape(k // 32, 32, n)
    amax = np.abs(w).max(1)
    if fmt == "e4m3":
        byte = np.frexp(amax)[1] - 1 + 127 - 7
    else:
        mant, ex = np.frexp(amax / 6.0)
        byte = np.where(mant > 0.5, ex, ex - 1) + 127
    byte = np.clip(np.where(amax > 0, byte, 1), 1, 254)
    scaled = (w * np.exp2(127.0 - byte)[:, None, :]).reshape(k, n).astype(np.float32)
    by_word = np.ascontiguousarray(scaled.reshape(k // 512, 128, 4, n).transpose(0, 1, 3, 2))
    if fmt == "e4m3":
        words = by_word.astype(ml_dtypes.float8_e4m3fn).view(np.uint8)
    else:
        c = by_word.astype(ml_dtypes.float4_e2m1fn).view(np.uint8) & 0xF
        words = c[..., 0::2] | (c[..., 1::2] << 4)
    return np.ascontiguousarray(words), np.ascontiguousarray(byte.astype(np.uint8).reshape(k // 512, 16, n))


def unpack_weight(words, scales, fmt):
    g, p, n, _ = words.shape
    if fmt == "e4m3":
        vals = np.ascontiguousarray(words).view(ml_dtypes.float8_e4m3fn).astype(np.float64)
    else:
        nib = np.empty((g, p, n, 4), np.uint8)
        nib[..., 0::2] = words & 0xF
        nib[..., 1::2] = words >> 4
        vals = E2M1[nib]
    vals = vals * np.repeat(np.exp2(scales.astype(np.float64) - 127.0), 8, axis=1)[..., None]
    return vals.transpose(0, 1, 3, 2).reshape(g * 512, n)

def pack4(w):
    words, scales = pack_weight(w, "e2m1")
    return words.reshape(words.shape[0], 128, -1), scales


def unpack4(words, scales):
    return unpack_weight(words.reshape(words.shape[0], 128, -1, 2), scales, "e2m1")


B, S, D, H, HKV, HD, WINDOW, KB = 1, 512, 2048, 16, 8, 128, 256, 512
EPS = 1e-6
THETA = 10000.0


def rope_tables():
    inv_freq = 1.0 / THETA ** (np.arange(0, HD, 2) / HD)
    ang = np.arange(S)[:, None] * inv_freq[None, :]
    emb = np.concatenate([ang, ang], axis=-1)
    return np.broadcast_to(np.cos(emb)[None], (B, S, HD)), np.broadcast_to(np.sin(emb)[None], (B, S, HD))


def rms_norm(x, gain):
    var = np.mean(x * x, axis=-1, keepdims=True)
    return x * (1.0 / np.sqrt(var + EPS)) * gain


def rotate_half(x):
    return np.concatenate([-x[..., HD // 2:], x[..., :HD // 2]], axis=-1)


def apply_rope(x, cos, sin):
    return x * cos[:, :, None, :] + rotate_half(x) * sin[:, :, None, :]


def setup_inputs():
    s = mx_kscale(D)
    cos, sin = rope_tables()
    hidden_states = bf(np.random.standard_normal((B, S, D)) * s)
    Wq_words, Wq_scales = pack4(np.random.standard_normal((D, H * HD)) / np.sqrt(D) / s[:, None])
    Wk_words, Wk_scales = pack4(np.random.standard_normal((D, HKV * HD)) / np.sqrt(D) / s[:, None])
    Wv_words, Wv_scales = pack4(np.random.standard_normal((D, HKV * HD)) * 2.0 / np.sqrt(D) / s[:, None])
    q_scale = bf(np.random.uniform(0.5, 1.5, HD))
    k_scale = bf(np.random.uniform(0.5, 1.5, HD))
    return {
        "hidden_states": hidden_states,
        "cos": bf(cos),
        "sin": bf(sin),
        "Wq_words": Wq_words,
        "Wq_scales": Wq_scales,
        "Wk_words": Wk_words,
        "Wk_scales": Wk_scales,
        "Wv_words": Wv_words,
        "Wv_scales": Wv_scales,
        "q_scale": q_scale,
        "k_scale": k_scale,
    }


def reference(hidden_states, cos, sin, Wq_words, Wq_scales, Wk_words, Wk_scales, Wv_words, Wv_scales, q_scale, k_scale):
    xq = mxq(f64(hidden_states), 2, "e4m3")
    q = (xq @ unpack4(Wq_words, Wq_scales)).reshape(B, S, H, HD)
    k = (xq @ unpack4(Wk_words, Wk_scales)).reshape(B, S, HKV, HD)
    v = (xq @ unpack4(Wv_words, Wv_scales)).reshape(B, S, HKV, HD)
    q = rms_norm(q, f64(q_scale))
    k = rms_norm(k, f64(k_scale))
    q = apply_rope(q, f64(cos), f64(sin))
    k = apply_rope(k, f64(cos), f64(sin))
    return q, k, v

@@ -1,0 +1,353 @@
+from contextlib import ExitStack
+
+import concourse.mybir as mybir
+from concourse.masks import make_identity
+
+F32 = mybir.dt.float32
+BF16 = mybir.dt.bfloat16
+I32 = mybir.dt.int32
+U32 = mybir.dt.uint32
+U8 = mybir.dt.uint8
+FP8X4 = mybir.dt.float8_e4m3fn_x4
+FP4X4 = mybir.dt.float4_e2m1fn_x4
+ALU = mybir.AluOpType
+ACT = mybir.ActivationFunctionType
+
+P = 128
+TOKENS = 512
+TOKEN_TILES = TOKENS // P
+D_MODEL = 2048
+PACK = 4
+K_PASS = P * PACK
+PASSES = D_MODEL // K_PASS
+HEAD = 128
+HALF = HEAD // 2
+BANK = 512
+BANK_HEADS = BANK // HEAD
+SLAB_BANKS = 2
+SLAB = SLAB_BANKS * BANK
+SLAB_HEADS = SLAB // HEAD
+EPS = 1e-6
+NORMED_SLABS = 3
+WARM_BEFORE = 5
+WARM_TILES = 2
+WARM_EACH = 2
+PLANE_SHIFT = 128
+CODES_SHIFT = 64
+SCALES_SHIFT = 192
+HELPED_UNITS = 1
+
+FLOPS = 2 * TOKENS * D_MODEL * (2048 + 1024 + 1024)
+
+
+def tile_multiheadattention_pa_kernel(
+    tc,
+    hidden_states,
+    cos,
+    sin,
+    Wq_words,
+    Wq_scales,
+    Wk_words,
+    Wk_scales,
+    Wv_words,
+    Wv_scales,
+    q_scale,
+    k_scale,
+    out_0,
+    out_1,
+    out_2,
+):
+    nc = tc.nc
+
+    x_dram = hidden_states[0].rearrange("(p m) d -> p m d", m=TOKEN_TILES)
+    cos_dram = cos[0].rearrange("(p m) j -> p m j", m=TOKEN_TILES)
+    sin_dram = sin[0].rearrange("(p m) j -> p m j", m=TOKEN_TILES)
+    q_dram = out_0[0].rearrange("(p m) h j -> p m (h j)", m=TOKEN_TILES)
+    k_dram = out_1[0].rearrange("(p m) h j -> p m (h j)", m=TOKEN_TILES)
+    v_dram = out_2[0].rearrange("(p m) h j -> p m (h j)", m=TOKEN_TILES)
+
+    slabs = (
+        {"words": Wq_words, "scales": Wq_scales, "first": 0, "out": q_dram, "gain": 0},
+        {"words": Wq_words, "scales": Wq_scales, "first": SLAB, "out": q_dram, "gain": 0},
+        {"words": Wk_words, "scales": Wk_scales, "first": 0, "out": k_dram, "gain": 1},
+        {"words": Wv_words, "scales": Wv_scales, "first": 0, "out": v_dram, "gain": None},
+    )
+
+    with ExitStack() as ctx:
+        ctx.enter_context(tc.manual_schedule())
+        resident = ctx.enter_context(tc.tile_pool(name="resident", bufs=1))
+        prep = ctx.enter_context(tc.tile_pool(name="prep", bufs=4))
+        small = ctx.enter_context(tc.tile_pool(name="small", bufs=6))
+        squares = ctx.enter_context(tc.tile_pool(name="squares", bufs=3))
+        products = ctx.enter_context(tc.tile_pool(name="products", bufs=6))
+        results = ctx.enter_context(tc.tile_pool(name="results", bufs=6))
+        copies = ctx.enter_context(tc.tile_pool(name="copies", bufs=4))
+        psum = ctx.enter_context(tc.psum_pool(name="psum", bufs=8))
+
+        w_words = []
+        w_planes = []
+
+        def zero_plane(s):
+            whole = resident.tile([P, PLANE_SHIFT + PASSES * SLAB], U8, align_bytes=256, name="plane%d" % s)
+            nc.vector.memset(whole[:].bitcast(I32), 0)
+            w_planes.append(whole[:, PLANE_SHIFT:].rearrange("p (g n) -> p g n", g=PASSES))
+            w_words.append(
+                [
+                    resident.tile([P, PASSES, 2 * BANK], U8, align_bytes=256, name="words%d_%d" % (s, b))
+                    for b in range(SLAB_BANKS)
+                ]
+            )
+
+        def load_scales(s, first, width):
+            rows = slabs[s]["scales"].bitcast(I32).rearrange("g (j r) n -> r j g n", r=4)
+            first_word = (slabs[s]["first"] + first) // 4
+            for r in range(4):
+                nc.sync.dma_start(
+                    out=w_planes[s][r:P:32, :, first : first + width].bitcast(I32),
+                    in_=rows[r, :, :, first_word : first_word + width // 4],
+                )
+
+        def load_words(s, b, first_pass, passes):
+            source = slabs[s]["words"].bitcast(I32).rearrange("g p w -> p g w")
+            first_word = (slabs[s]["first"] + b * BANK) // 2
+            nc.sync.dma_start(
+                out=w_words[s][b][:, first_pass : first_pass + passes, :].bitcast(I32),
+                in_=source[:, first_pass : first_pass + passes, first_word : first_word + BANK // 2],
+            )
+
+        ones = resident.tile([P, P], BF16, name="ones")
+        nc.vector.memset(ones[:], 1.0)
+        filler = resident.tile([P, BANK], BF16, name="filler")
+        nc.vector.memset(filler[:], 0.0)
+
+        def keep_warm(count):
+            for i in range(count):
+                idle = psum.tile([P, BANK], F32, tag="bank", name="idle")
+                nc.tensor.matmul(out=idle[:], lhsT=ones[:], rhs=filler[:], start=True, stop=True)
+
+        gain_rows = resident.tile([P, 2 * HEAD], BF16, name="gain_rows")
+        nc.vector.memset(gain_rows[:], 0.0)
+        eps = resident.tile([P, 1], F32, name="eps")
+        nc.vector.memset(eps[:], EPS)
+        ident = resident.tile([P, P], F32, name="ident")
+        make_identity(nc, ident[:])
+        for s in range(len(slabs)):
+            zero_plane(s)
+
+        x_sb = []
+        for m in range(TOKEN_TILES):
+            x_tile = resident.tile([P, D_MODEL], BF16, name="x%d" % m)
+            x_sb.append(x_tile)
+        for half in range(2):
+            columns = slice(half * D_MODEL // 2, (half + 1) * D_MODEL // 2)
+            nc.sync.dma_start(out=x_sb[0][:, columns], in_=x_dram[:, 0, columns])
+        nc.sync.dma_start(out=gain_rows[0:1, 0:HEAD], in_=q_scale.unsqueeze(0))
+        nc.sync.dma_start(out=gain_rows[0:1, HEAD : 2 * HEAD], in_=k_scale.unsqueeze(0))
+        for m in range(1, TOKEN_TILES):
+            nc.sync.dma_start(out=x_sb[m][:], in_=x_dram[:, m, :])
+        load_scales(0, 0, SLAB)
+        load_words(0, 0, 0, PASSES // 2)
+        load_words(0, 0, PASSES // 2, PASSES // 2)
+        load_words(0, 1, 0, PASSES)
+        cos_sb = resident.tile([P, TOKEN_TILES, HEAD], BF16, name="cos_sb")
+        nc.sync.dma_start(out=cos_sb[:], in_=cos_dram)
+        sin_sb = resident.tile([P, TOKEN_TILES, HEAD], BF16, name="sin_sb")
+        nc.sync.dma_start(out=sin_sb[:], in_=sin_dram)
+        for s in range(1, len(slabs)):
+            load_scales(s, 0, SLAB)
+            for b in range(SLAB_BANKS):
+                load_words(s, b, 0, PASSES)
+
+        warm = resident.tile([P, 1], F32, name="warm")
+        nc.scalar.activation(out=warm[:], in_=eps[:], func=ACT.Abs_reciprocal_sqrt)
+
+        tables = [
+            resident.tile([P, TOKEN_TILES, 2, HEAD], F32, name="table%d" % w) for w in range(2)
+        ]
+        gain_k = resident.tile([P, 2, HALF], F32, name="gain_k")
+        turn_k = resident.tile([P, 2, HALF], F32, name="turn_k")
+
+        def build_tables():
+            gain_ps = psum.tile([P, BANK], F32, tag="bank", name="gain_ps")
+            nc.tensor.matmul(
+                out=gain_ps[:, 0 : 2 * HEAD], lhsT=ones[:], rhs=gain_rows[:], start=True, stop=True
+            )
+            spread_k = gain_ps[:, HEAD : 2 * HEAD].rearrange("p (a j) -> p a j", a=2)
+            nc.scalar.copy(out=gain_k[:], in_=spread_k)
+            nc.scalar.copy(out=turn_k[:, 0, :], in_=spread_k[:, 0, :])
+            nc.scalar.mul(out=turn_k[:, 1, :], in_=spread_k[:, 1, :], mul=-1.0)
+
+            nc.vector.tensor_tensor(
+                out=tables[0][:, :, 0, :],
+                in0=cos_sb[:],
+                in1=gain_ps[:, 0:HEAD].unsqueeze(1).to_broadcast([P, TOKEN_TILES, HEAD]),
+                op=ALU.mult,
+            )
+            nc.vector.tensor_tensor(
+                out=tables[0][:, :, 1, 0:HALF],
+                in0=sin_sb[:, :, HALF:HEAD],
+                in1=gain_ps[:, 0:HALF].unsqueeze(1).to_broadcast([P, TOKEN_TILES, HALF]),
+                op=ALU.mult,
+            )
+            nc.vector.scalar_tensor_tensor(
+                out=tables[0][:, :, 1, HALF:HEAD],
+                in0=sin_sb[:, :, 0:HALF],
+                scalar=-1.0,
+                in1=gain_ps[:, HALF:HEAD].unsqueeze(1).to_broadcast([P, TOKEN_TILES, HALF]),
+                op0=ALU.mult,
+                op1=ALU.mult,
+            )
+
+            shape = [P, TOKEN_TILES, 2, HALF]
+            nc.gpsimd.tensor_tensor(
+                out=tables[1][:, :, 0, :].rearrange("p m (a j) -> p m a j", a=2),
+                in0=cos_sb[:].rearrange("p m (a j) -> p m a j", a=2),
+                in1=gain_k[:].unsqueeze(1).to_broadcast(shape),
+                op=ALU.mult,
+            )
+            nc.gpsimd.tensor_tensor(
+                out=tables[1][:, :, 1, :].rearrange("p m (a j) -> p m a j", a=2),
+                in0=sin_sb[:].rearrange("p m (a j) -> p m a j", a=2)[:, :, ::-1, :],
+                in1=turn_k[:].unsqueeze(1).to_broadcast(shape),
+                op=ALU.mult,
+            )
+
+        x_codes = []
+        x_scales = []
+        keep_warm(WARM_BEFORE)
+        for m in range(TOKEN_TILES):
+            x_pairs = x_sb[m][:].bitcast(F32)
+            grouped = prep.tile([P, PASSES, P, PACK], BF16, align_bytes=64, name="grouped")
+            grouped_pairs = grouped[:].bitcast(F32)
+            for b in range(2):
+                xt = psum.tile([P, 2, 2, P], F32, tag="bank", name="xt")
+                for i in range(2):
+                    g = 2 * b + i
+                    for u in range(2):
+                        nc.tensor.transpose(
+                            out=xt[:, i, u, :],
+                            in_=x_pairs[:, 256 * g + u : 256 * (g + 1) : 2],
+                            identity=ident[:],
+                        )
+                nc.scalar.copy(
+                    out=grouped_pairs[:, 2 * b : 2 * b + 2, :, :],
+                    in_=xt[:].rearrange("p i u r -> p i r u"),
+                )
+            if m >= TOKEN_TILES - WARM_TILES:
+                keep_warm(WARM_EACH)
+            codes = resident.tile([P, CODES_SHIFT // 4 + PASSES * P], U32, align_bytes=256, name="x_codes%d" % m)
+            scales = resident.tile([P, SCALES_SHIFT + PASSES * P], U8, align_bytes=256, name="x_scales%d" % m)
+            nc.vector.quantize_mx(
+                out=codes[:, CODES_SHIFT // 4 :].bitcast(FP8X4),
+                scales=scales[:, SCALES_SHIFT:],
+                in_=grouped[:].rearrange("p g r t -> p (g r t)"),
+            )
+            x_codes.append(codes[:, CODES_SHIFT // 4 :].rearrange("p (g r) -> p g r", g=PASSES))
+            x_scales.append(scales[:, SCALES_SHIFT:].rearrange("p (g r) -> p g r", g=PASSES))
+        build_tables()
+
+        def project(s, m, b):
+            acc = psum.tile([P, BANK], F32, tag="bank", name="acc")
+            for g in range(PASSES):
+                nc.tensor.matmul_mx(
+                    out=acc[:],
+                    lhsT=x_codes[m][:, g, :].bitcast(FP8X4),
+                    lhsT_scale=x_scales[m][:, g, :],
+                    rhs=w_words[s][b][:, g, :].bitcast(FP4X4),
+                    rhs_scale=w_planes[s][:, g, BANK * b : BANK * (b + 1)],
+                    start=(g == 0),
+                    stop=(g == PASSES - 1),
+                )
+            return acc
+
+        def square_sums(acc):
+            squared = squares.tile([P, BANK_HEADS, HEAD], F32, name="squared")
+            sums = small.tile([P, BANK_HEADS], F32, name="sums")
+            for h in range(BANK_HEADS):
+                nc.scalar.activation(
+                    out=squared[:, h, :],
+                    in_=acc[:, h * HEAD : (h + 1) * HEAD],
+                    func=ACT.Square,
+                    accum_out=sums[:, h : h + 1],
+                )
+            return sums
+
+        def norm_and_turn(s, m, b, acc, sums, shares):
+            inv_rms = small.tile([P, BANK_HEADS], F32, name="inv_rms")
+            nc.scalar.activation(
+                out=inv_rms[:],
+                in_=sums[:],
+                func=ACT.Abs_reciprocal_sqrt,
+                scale=1.0 / HEAD,
+                bias=eps[:],
+            )
+            for h in range(BANK_HEADS):
+                nc.vector.scalar_tensor_tensor(
+                    out=shares[:, b * BANK_HEADS + h, :, :],
+                    in0=acc[:, h * HEAD : (h + 1) * HEAD].unsqueeze(1).to_broadcast([P, 2, HEAD]),
+                    scalar=inv_rms[:, h : h + 1],
+                    in1=tables[slabs[s]["gain"]][:, m, :, :],
+                    op0=ALU.mult,
+                    op1=ALU.mult,
+                )
+
+        def add_and_store(s, m, shares):
+            slab = slabs[s]
+            result = results.tile([P, SLAB_HEADS, HEAD], F32, name="result")
+            total = result[:].rearrange("p h (a j) -> p h a j", a=2)
+            own = shares[:, :, 0, :].rearrange("p h (a j) -> p h a j", a=2)
+            other = shares[:, :, 1, :].rearrange("p h (a j) -> p h a j", a=2)[:, :, ::-1, :]
+            units_left = (NORMED_SLABS - s) * TOKEN_TILES - m
+            if units_left <= HELPED_UNITS:
+                nc.gpsimd.tensor_tensor(
+                    out=total[:, 0:BANK_HEADS], in0=own[:, 0:BANK_HEADS], in1=other[:, 0:BANK_HEADS], op=ALU.add
+                )
+                nc.vector.tensor_tensor(
+                    out=total[:, BANK_HEADS:], in0=own[:, BANK_HEADS:], in1=other[:, BANK_HEADS:], op=ALU.add
+                )
+            else:
+                nc.gpsimd.tensor_tensor(out=total, in0=own, in1=other, op=ALU.add)
+            nc.sync.dma_start(
+                out=slab["out"][:, m, slab["first"] : slab["first"] + SLAB],
+                in_=result[:].rearrange("p h j -> p (h j)"),
+            )
+
+        order = [(s, m, b) for s in range(len(slabs)) for m in range(TOKEN_TILES) for b in range(SLAB_BANKS)]
+        open_units = {}
+        waiting = []
+
+        def finish_waiting():
+            for s, m, b, acc, sums, shares in waiting:
+                norm_and_turn(s, m, b, acc, sums, shares)
+                if b == SLAB_BANKS - 1:
+                    add_and_store(s, m, shares)
+            waiting.clear()
+
+        for s, m, b in order:
+            acc = project(s, m, b)
+            if slabs[s]["gain"] is None:
+                finish_waiting()
+                if b == 0:
+                    copied = copies.tile([P, SLAB], F32, name="copied")
+                    open_units[(s, m)] = copied
+                copied = open_units[(s, m)]
+                if m < TOKEN_TILES - 1:
+                    nc.scalar.copy(out=copied[:, b * BANK : (b + 1) * BANK], in_=acc[:])
+                    if b == SLAB_BANKS - 1:
+                        nc.scalar.dma_start(out=slabs[s]["out"][:, m, :], in_=copied[:])
+                else:
+                    parts = 1 if b == 0 else 2
+                    for part in range(parts):
+                        first = b * BANK + part * BANK // parts
+                        columns = slice(first, first + BANK // parts)
+                        nc.scalar.copy(out=copied[:, columns], in_=acc[:, first - b * BANK : first - b * BANK + BANK // parts])
+                        queue = nc.scalar if (b == SLAB_BANKS - 1 and part == parts - 1) else nc.sync
+                        queue.dma_start(out=slabs[s]["out"][:, m, columns], in_=copied[:, columns])
+            else:
+                if b == 0:
+                    shares = products.tile([P, SLAB_HEADS, 2, HEAD], F32, name="shares")
+                    open_units[(s, m)] = shares
+                shares = open_units[(s, m)]
+                sums = square_sums(acc)
+                finish_waiting()
+                waiting.append((s, m, b, acc, sums, shares))

@@ -37,6 +37,8 @@ CODES_SHIFT = 64
 SCALES_SHIFT = 192
 HELPED_UNITS = 1
 
+LOAD_BEHIND = {(0, 0): 2, (0, 3): 3}
+
 FLOPS = 2 * TOKENS * D_MODEL * (2048 + 1024 + 1024)
 
 
@@ -80,7 +82,7 @@ def tile_multiheadattention_pa_kernel(
         small = ctx.enter_context(tc.tile_pool(name="small", bufs=6))
         squares = ctx.enter_context(tc.tile_pool(name="squares", bufs=3))
         products = ctx.enter_context(tc.tile_pool(name="products", bufs=6))
-        results = ctx.enter_context(tc.tile_pool(name="results", bufs=6))
+        results = ctx.enter_context(tc.tile_pool(name="results", bufs=8))
         copies = ctx.enter_context(tc.tile_pool(name="copies", bufs=4))
         psum = ctx.enter_context(tc.psum_pool(name="psum", bufs=8))
 
@@ -153,10 +155,13 @@ def tile_multiheadattention_pa_kernel(
         nc.sync.dma_start(out=cos_sb[:], in_=cos_dram)
         sin_sb = resident.tile([P, TOKEN_TILES, HEAD], BF16, name="sin_sb")
         nc.sync.dma_start(out=sin_sb[:], in_=sin_dram)
-        for s in range(1, len(slabs)):
+
+        def load_slab(s):
             load_scales(s, 0, SLAB)
             for b in range(SLAB_BANKS):
                 load_words(s, b, 0, PASSES)
+
+        load_slab(1)
 
         warm = resident.tile([P, 1], F32, name="warm")
         nc.scalar.activation(out=warm[:], in_=eps[:], func=ACT.Abs_reciprocal_sqrt)
@@ -321,6 +326,8 @@ def tile_multiheadattention_pa_kernel(
                 norm_and_turn(s, m, b, acc, sums, shares)
                 if b == SLAB_BANKS - 1:
                     add_and_store(s, m, shares)
+                    if (s, m) in LOAD_BEHIND:
+                        load_slab(LOAD_BEHIND[(s, m)])
             waiting.clear()
 
         for s, m, b in order:

@@ -37,7 +37,7 @@ CODES_SHIFT = 64
 SCALES_SHIFT = 192
 HELPED_UNITS = 1
 
-LOAD_BEHIND = {(0, 0): 2, (0, 3): 3}
+LOAD_BEHIND = {(0, 1, 0): 2, (0, 3, 1): 3}
 
 FLOPS = 2 * TOKENS * D_MODEL * (2048 + 1024 + 1024)
 
@@ -82,6 +82,7 @@ def tile_multiheadattention_pa_kernel(
         small = ctx.enter_context(tc.tile_pool(name="small", bufs=6))
         squares = ctx.enter_context(tc.tile_pool(name="squares", bufs=3))
         products = ctx.enter_context(tc.tile_pool(name="products", bufs=6))
+        halves = ctx.enter_context(tc.tile_pool(name="halves", bufs=8))
         results = ctx.enter_context(tc.tile_pool(name="results", bufs=8))
         copies = ctx.enter_context(tc.tile_pool(name="copies", bufs=4))
         psum = ctx.enter_context(tc.psum_pool(name="psum", bufs=8))
@@ -150,11 +151,11 @@ def tile_multiheadattention_pa_kernel(
         load_scales(0, 0, SLAB)
         load_words(0, 0, 0, PASSES // 2)
         load_words(0, 0, PASSES // 2, PASSES // 2)
-        load_words(0, 1, 0, PASSES)
         cos_sb = resident.tile([P, TOKEN_TILES, HEAD], BF16, name="cos_sb")
         nc.sync.dma_start(out=cos_sb[:], in_=cos_dram)
         sin_sb = resident.tile([P, TOKEN_TILES, HEAD], BF16, name="sin_sb")
         nc.sync.dma_start(out=sin_sb[:], in_=sin_dram)
+        load_words(0, 1, 0, PASSES)
 
         def load_slab(s):
             load_scales(s, 0, SLAB)
@@ -296,6 +297,22 @@ def tile_multiheadattention_pa_kernel(
                     op1=ALU.mult,
                 )
 
+        def add_and_store_bank(s, m, b, shares):
+            slab = slabs[s]
+            half = halves.tile([P, BANK_HEADS, HEAD], F32, name="half")
+            heads = shares[:, b * BANK_HEADS : (b + 1) * BANK_HEADS]
+            nc.gpsimd.tensor_tensor(
+                out=half[:].rearrange("p h (a j) -> p h a j", a=2),
+                in0=heads[:, :, 0, :].rearrange("p h (a j) -> p h a j", a=2),
+                in1=heads[:, :, 1, :].rearrange("p h (a j) -> p h a j", a=2)[:, :, ::-1, :],
+                op=ALU.add,
+            )
+            column = slab["first"] + b * BANK
+            nc.sync.dma_start(
+                out=slab["out"][:, m, column : column + BANK],
+                in_=half[:].rearrange("p h j -> p (h j)"),
+            )
+
         def add_and_store(s, m, shares):
             slab = slabs[s]
             result = results.tile([P, SLAB_HEADS, HEAD], F32, name="result")
@@ -317,17 +334,20 @@ def tile_multiheadattention_pa_kernel(
                 in_=result[:].rearrange("p h j -> p (h j)"),
             )
 
-        order = [(s, m, b) for s in range(len(slabs)) for m in range(TOKEN_TILES) for b in range(SLAB_BANKS)]
+        order = [(0, m, b) for b in range(SLAB_BANKS) for m in range(TOKEN_TILES)]
+        order += [(s, m, b) for s in range(1, len(slabs)) for m in range(TOKEN_TILES) for b in range(SLAB_BANKS)]
         open_units = {}
         waiting = []
 
         def finish_waiting():
             for s, m, b, acc, sums, shares in waiting:
                 norm_and_turn(s, m, b, acc, sums, shares)
-                if b == SLAB_BANKS - 1:
+                if s == 0:
+                    add_and_store_bank(s, m, b, shares)
+                elif b == SLAB_BANKS - 1:
                     add_and_store(s, m, shares)
-                    if (s, m) in LOAD_BEHIND:
-                        load_slab(LOAD_BEHIND[(s, m)])
+                if (s, m, b) in LOAD_BEHIND:
+                    load_slab(LOAD_BEHIND[(s, m, b)])
             waiting.clear()
 
         for s, m, b in order:

@@ -29,8 +29,8 @@ SLAB = SLAB_BANKS * BANK
 SLAB_HEADS = SLAB // HEAD
 EPS = 1e-6
 NORMED_SLABS = 3
-WARM_BEFORE = 5
-WARM_TILES = 2
+WARM_BEFORE = 3
+WARM_BEHIND = 2
 WARM_EACH = 2
 PLANE_SHIFT = 128
 CODES_SHIFT = 64
@@ -90,10 +90,14 @@ def tile_multiheadattention_pa_kernel(
         w_words = []
         w_planes = []
 
-        def zero_plane(s):
-            whole = resident.tile([P, PLANE_SHIFT + PASSES * SLAB], U8, align_bytes=256, name="plane%d" % s)
-            nc.vector.memset(whole[:].bitcast(I32), 0)
-            w_planes.append(whole[:, PLANE_SHIFT:].rearrange("p (g n) -> p g n", g=PASSES))
+        def zero_plane(s, parts):
+            planes = []
+            for i in range(parts):
+                width = SLAB // parts
+                whole = resident.tile([P, PLANE_SHIFT + PASSES * width], U8, align_bytes=256, name="plane%d_%d" % (s, i))
+                nc.vector.memset(whole[:].bitcast(I32), 0)
+                planes.append(whole[:, PLANE_SHIFT:].rearrange("p (g n) -> p g n", g=PASSES))
+            w_planes.append(planes)
             w_words.append(
                 [
                     resident.tile([P, PASSES, 2 * BANK], U8, align_bytes=256, name="words%d_%d" % (s, b))
@@ -101,12 +105,13 @@ def tile_multiheadattention_pa_kernel(
                 ]
             )
 
-        def load_scales(s, first, width):
+        def load_scales(s, part):
             rows = slabs[s]["scales"].bitcast(I32).rearrange("g (j r) n -> r j g n", r=4)
-            first_word = (slabs[s]["first"] + first) // 4
+            width = SLAB // len(w_planes[s])
+            first_word = (slabs[s]["first"] + part * width) // 4
             for r in range(4):
                 nc.sync.dma_start(
-                    out=w_planes[s][r:P:32, :, first : first + width].bitcast(I32),
+                    out=w_planes[s][part][r:P:32, :, :].bitcast(I32),
                     in_=rows[r, :, :, first_word : first_word + width // 4],
                 )
 
@@ -135,30 +140,31 @@ def tile_multiheadattention_pa_kernel(
         ident = resident.tile([P, P], F32, name="ident")
         make_identity(nc, ident[:])
         for s in range(len(slabs)):
-            zero_plane(s)
+            zero_plane(s, SLAB_BANKS if s == 0 else 1)
 
         x_sb = []
         for m in range(TOKEN_TILES):
             x_tile = resident.tile([P, D_MODEL], BF16, name="x%d" % m)
             x_sb.append(x_tile)
-        for half in range(2):
-            columns = slice(half * D_MODEL // 2, (half + 1) * D_MODEL // 2)
-            nc.sync.dma_start(out=x_sb[0][:, columns], in_=x_dram[:, 0, columns])
-        nc.sync.dma_start(out=gain_rows[0:1, 0:HEAD], in_=q_scale.unsqueeze(0))
-        nc.sync.dma_start(out=gain_rows[0:1, HEAD : 2 * HEAD], in_=k_scale.unsqueeze(0))
-        for m in range(1, TOKEN_TILES):
-            nc.sync.dma_start(out=x_sb[m][:], in_=x_dram[:, m, :])
-        load_scales(0, 0, SLAB)
+        for m in range(TOKEN_TILES):
+            for half in range(2):
+                columns = slice(half * D_MODEL // 2, (half + 1) * D_MODEL // 2)
+                nc.sync.dma_start(out=x_sb[m][:, columns], in_=x_dram[:, m, columns])
+            if m == 0:
+                nc.sync.dma_start(out=gain_rows[0:1, 0:HEAD], in_=q_scale.unsqueeze(0))
+                nc.sync.dma_start(out=gain_rows[0:1, HEAD : 2 * HEAD], in_=k_scale.unsqueeze(0))
+        load_scales(0, 0)
         load_words(0, 0, 0, PASSES // 2)
         load_words(0, 0, PASSES // 2, PASSES // 2)
         cos_sb = resident.tile([P, TOKEN_TILES, HEAD], BF16, name="cos_sb")
         nc.sync.dma_start(out=cos_sb[:], in_=cos_dram)
         sin_sb = resident.tile([P, TOKEN_TILES, HEAD], BF16, name="sin_sb")
         nc.sync.dma_start(out=sin_sb[:], in_=sin_dram)
+        load_scales(0, 1)
         load_words(0, 1, 0, PASSES)
 
         def load_slab(s):
-            load_scales(s, 0, SLAB)
+            load_scales(s, 0)
             for b in range(SLAB_BANKS):
                 load_words(s, b, 0, PASSES)
 
@@ -239,7 +245,7 @@ def tile_multiheadattention_pa_kernel(
                     out=grouped_pairs[:, 2 * b : 2 * b + 2, :, :],
                     in_=xt[:].rearrange("p i u r -> p i r u"),
                 )
-            if m >= TOKEN_TILES - WARM_TILES:
+            if m == WARM_BEHIND:
                 keep_warm(WARM_EACH)
             codes = resident.tile([P, CODES_SHIFT // 4 + PASSES * P], U32, align_bytes=256, name="x_codes%d" % m)
             scales = resident.tile([P, SCALES_SHIFT + PASSES * P], U8, align_bytes=256, name="x_scales%d" % m)
@@ -253,6 +259,8 @@ def tile_multiheadattention_pa_kernel(
         build_tables()
 
         def project(s, m, b):
+            columns = slice(BANK * b, BANK * (b + 1))
+            planes = w_planes[s][0][:, :, columns] if len(w_planes[s]) == 1 else w_planes[s][b]
             acc = psum.tile([P, BANK], F32, tag="bank", name="acc")
             for g in range(PASSES):
                 nc.tensor.matmul_mx(
@@ -260,7 +268,7 @@ def tile_multiheadattention_pa_kernel(
                     lhsT=x_codes[m][:, g, :].bitcast(FP8X4),
                     lhsT_scale=x_scales[m][:, g, :],
                     rhs=w_words[s][b][:, g, :].bitcast(FP4X4),
-                    rhs_scale=w_planes[s][:, g, BANK * b : BANK * (b + 1)],
+                    rhs_scale=planes[:, g, :],
                     start=(g == 0),
                     stop=(g == PASSES - 1),
                 )
@@ -378,3 +386,5 @@ def tile_multiheadattention_pa_kernel(
                 sums = square_sums(acc)
                 finish_waiting()
                 waiting.append((s, m, b, acc, sums, shares))
+                if (s, m, b) == order[0]:
+                    finish_waiting()

@@ -35,7 +35,7 @@ WARM_EACH = 2
 PLANE_SHIFT = 128
 CODES_SHIFT = 64
 SCALES_SHIFT = 192
-HELPED_UNITS = 1
+HELPED_UNITS = 2
 
 LOAD_BEHIND = {(0, 1, 0): 2, (0, 3, 1): 3}
 
@@ -322,21 +322,20 @@ def tile_multiheadattention_pa_kernel(
             )
 
         def add_and_store(s, m, shares):
-            slab = slabs[s]
             result = results.tile([P, SLAB_HEADS, HEAD], F32, name="result")
-            total = result[:].rearrange("p h (a j) -> p h a j", a=2)
-            own = shares[:, :, 0, :].rearrange("p h (a j) -> p h a j", a=2)
-            other = shares[:, :, 1, :].rearrange("p h (a j) -> p h a j", a=2)[:, :, ::-1, :]
-            units_left = (NORMED_SLABS - s) * TOKEN_TILES - m
-            if units_left <= HELPED_UNITS:
-                nc.gpsimd.tensor_tensor(
-                    out=total[:, 0:BANK_HEADS], in0=own[:, 0:BANK_HEADS], in1=other[:, 0:BANK_HEADS], op=ALU.add
-                )
-                nc.vector.tensor_tensor(
-                    out=total[:, BANK_HEADS:], in0=own[:, BANK_HEADS:], in1=other[:, BANK_HEADS:], op=ALU.add
-                )
-            else:
-                nc.gpsimd.tensor_tensor(out=total, in0=own, in1=other, op=ALU.add)
+            add(nc.gpsimd, result, shares, 0, SLAB_HEADS)
+            store_unit(s, m, result)
+
+        def add(engine, result, shares, first, end):
+            engine.tensor_tensor(
+                out=result[:, first:end].rearrange("p h (a j) -> p h a j", a=2),
+                in0=shares[:, first:end, 0, :].rearrange("p h (a j) -> p h a j", a=2),
+                in1=shares[:, first:end, 1, :].rearrange("p h (a j) -> p h a j", a=2)[:, :, ::-1, :],
+                op=ALU.add,
+            )
+
+        def store_unit(s, m, result):
+            slab = slabs[s]
             nc.sync.dma_start(
                 out=slab["out"][:, m, slab["first"] : slab["first"] + SLAB],
                 in_=result[:].rearrange("p h j -> p (h j)"),
@@ -346,12 +345,23 @@ def tile_multiheadattention_pa_kernel(
         order += [(s, m, b) for s in range(1, len(slabs)) for m in range(TOKEN_TILES) for b in range(SLAB_BANKS)]
         open_units = {}
         waiting = []
+        half_done = []
 
         def finish_waiting():
             for s, m, b, acc, sums, shares in waiting:
                 norm_and_turn(s, m, b, acc, sums, shares)
+                units_left = (NORMED_SLABS - s) * TOKEN_TILES - m
                 if s == 0:
                     add_and_store_bank(s, m, b, shares)
+                elif units_left <= HELPED_UNITS:
+                    if b == 0:
+                        result = results.tile([P, SLAB_HEADS, HEAD], F32, name="result")
+                        add(nc.gpsimd, result, shares, 0, BANK_HEADS)
+                        half_done.append((s, m, result, shares))
+                    elif units_left == 1:
+                        for left_s, left_m, left_result, left_shares in half_done:
+                            add(nc.vector, left_result, left_shares, BANK_HEADS, SLAB_HEADS)
+                            store_unit(left_s, left_m, left_result)
                 elif b == SLAB_BANKS - 1:
                     add_and_store(s, m, shares)
                 if (s, m, b) in LOAD_BEHIND:
@@ -368,7 +378,10 @@ def tile_multiheadattention_pa_kernel(
                 copied = open_units[(s, m)]
                 if m < TOKEN_TILES - 1:
                     nc.scalar.copy(out=copied[:, b * BANK : (b + 1) * BANK], in_=acc[:])
-                    if b == SLAB_BANKS - 1:
+                    if m == 0:
+                        columns = slice(b * BANK, (b + 1) * BANK)
+                        nc.scalar.dma_start(out=slabs[s]["out"][:, m, columns], in_=copied[:, columns])
+                    elif b == SLAB_BANKS - 1:
                         nc.scalar.dma_start(out=slabs[s]["out"][:, m, :], in_=copied[:])
                 else:
                     parts = 1 if b == 0 else 2

@@ -29,9 +29,8 @@ SLAB = SLAB_BANKS * BANK
 SLAB_HEADS = SLAB // HEAD
 EPS = 1e-6
 NORMED_SLABS = 3
-WARM_BEFORE = 3
-WARM_BEHIND = 2
-WARM_EACH = 2
+WARM_UNTIL = 6
+WARM_BEFORE = 4
 PLANE_SHIFT = 128
 CODES_SHIFT = 64
 SCALES_SHIFT = 192
@@ -245,8 +244,9 @@ def tile_multiheadattention_pa_kernel(
                     out=grouped_pairs[:, 2 * b : 2 * b + 2, :, :],
                     in_=xt[:].rearrange("p i u r -> p i r u"),
                 )
-            if m == WARM_BEHIND:
-                keep_warm(WARM_EACH)
+                half_tile = 2 * m + b
+                if half_tile % 3 > 0 and half_tile < WARM_UNTIL:
+                    keep_warm(1)
             codes = resident.tile([P, CODES_SHIFT // 4 + PASSES * P], U32, align_bytes=256, name="x_codes%d" % m)
             scales = resident.tile([P, SCALES_SHIFT + PASSES * P], U8, align_bytes=256, name="x_scales%d" % m)
             nc.vector.quantize_mx(

from contextlib import ExitStack

import concourse.mybir as mybir
from concourse.masks import make_identity

F32 = mybir.dt.float32
BF16 = mybir.dt.bfloat16
I32 = mybir.dt.int32
U32 = mybir.dt.uint32
U8 = mybir.dt.uint8
FP8X4 = mybir.dt.float8_e4m3fn_x4
FP4X4 = mybir.dt.float4_e2m1fn_x4
ALU = mybir.AluOpType
ACT = mybir.ActivationFunctionType

P = 128
TOKENS = 512
TOKEN_TILES = TOKENS // P
D_MODEL = 2048
PACK = 4
K_PASS = P * PACK
PASSES = D_MODEL // K_PASS
HEAD = 128
HALF = HEAD // 2
BANK = 512
BANK_HEADS = BANK // HEAD
SLAB_BANKS = 2
SLAB = SLAB_BANKS * BANK
SLAB_HEADS = SLAB // HEAD
EPS = 1e-6
NORMED_SLABS = 3
WARM_UNTIL = 6
WARM_BEFORE = 4
PLANE_SHIFT = 128
CODES_SHIFT = 64
SCALES_SHIFT = 192
HELPED_UNITS = 2

LOAD_BEHIND = {(0, 1, 0): 2, (0, 3, 1): 3}

FLOPS = 2 * TOKENS * D_MODEL * (2048 + 1024 + 1024)


def tile_multiheadattention_pa_kernel(
    tc,
    hidden_states,
    cos,
    sin,
    Wq_words,
    Wq_scales,
    Wk_words,
    Wk_scales,
    Wv_words,
    Wv_scales,
    q_scale,
    k_scale,
    out_0,
    out_1,
    out_2,
):
    nc = tc.nc

    x_dram = hidden_states[0].rearrange("(p m) d -> p m d", m=TOKEN_TILES)
    cos_dram = cos[0].rearrange("(p m) j -> p m j", m=TOKEN_TILES)
    sin_dram = sin[0].rearrange("(p m) j -> p m j", m=TOKEN_TILES)
    q_dram = out_0[0].rearrange("(p m) h j -> p m (h j)", m=TOKEN_TILES)
    k_dram = out_1[0].rearrange("(p m) h j -> p m (h j)", m=TOKEN_TILES)
    v_dram = out_2[0].rearrange("(p m) h j -> p m (h j)", m=TOKEN_TILES)

    slabs = (
        {"words": Wq_words, "scales": Wq_scales, "first": 0, "out": q_dram, "gain": 0},
        {"words": Wq_words, "scales": Wq_scales, "first": SLAB, "out": q_dram, "gain": 0},
        {"words": Wk_words, "scales": Wk_scales, "first": 0, "out": k_dram, "gain": 1},
        {"words": Wv_words, "scales": Wv_scales, "first": 0, "out": v_dram, "gain": None},
    )

    with ExitStack() as ctx:
        ctx.enter_context(tc.manual_schedule())
        resident = ctx.enter_context(tc.tile_pool(name="resident", bufs=1))
        prep = ctx.enter_context(tc.tile_pool(name="prep", bufs=4))
        small = ctx.enter_context(tc.tile_pool(name="small", bufs=6))
        squares = ctx.enter_context(tc.tile_pool(name="squares", bufs=3))
        products = ctx.enter_context(tc.tile_pool(name="products", bufs=6))
        halves = ctx.enter_context(tc.tile_pool(name="halves", bufs=8))
        results = ctx.enter_context(tc.tile_pool(name="results", bufs=8))
        copies = ctx.enter_context(tc.tile_pool(name="copies", bufs=4))
        psum = ctx.enter_context(tc.psum_pool(name="psum", bufs=8))

        w_words = []
        w_planes = []

        def zero_plane(s, parts):
            planes = []
            for i in range(parts):
                width = SLAB // parts
                whole = resident.tile([P, PLANE_SHIFT + PASSES * width], U8, align_bytes=256, name="plane%d_%d" % (s, i))
                nc.vector.memset(whole[:].bitcast(I32), 0)
                planes.append(whole[:, PLANE_SHIFT:].rearrange("p (g n) -> p g n", g=PASSES))
            w_planes.append(planes)
            w_words.append(
                [
                    resident.tile([P, PASSES, 2 * BANK], U8, align_bytes=256, name="words%d_%d" % (s, b))
                    for b in range(SLAB_BANKS)
                ]
            )

        def load_scales(s, part):
            rows = slabs[s]["scales"].bitcast(I32).rearrange("g (j r) n -> r j g n", r=4)
            width = SLAB // len(w_planes[s])
            first_word = (slabs[s]["first"] + part * width) // 4
            for r in range(4):
                nc.sync.dma_start(
                    out=w_planes[s][part][r:P:32, :, :].bitcast(I32),
                    in_=rows[r, :, :, first_word : first_word + width // 4],
                )

        def load_words(s, b, first_pass, passes):
            source = slabs[s]["words"].bitcast(I32).rearrange("g p w -> p g w")
            first_word = (slabs[s]["first"] + b * BANK) // 2
            nc.sync.dma_start(
                out=w_words[s][b][:, first_pass : first_pass + passes, :].bitcast(I32),
                in_=source[:, first_pass : first_pass + passes, first_word : first_word + BANK // 2],
            )

        ones = resident.tile([P, P], BF16, name="ones")
        nc.vector.memset(ones[:], 1.0)
        filler = resident.tile([P, BANK], BF16, name="filler")
        nc.vector.memset(filler[:], 0.0)

        def keep_warm(count):
            for i in range(count):
                idle = psum.tile([P, BANK], F32, tag="bank", name="idle")
                nc.tensor.matmul(out=idle[:], lhsT=ones[:], rhs=filler[:], start=True, stop=True)

        gain_rows = resident.tile([P, 2 * HEAD], BF16, name="gain_rows")
        nc.vector.memset(gain_rows[:], 0.0)
        eps = resident.tile([P, 1], F32, name="eps")
        nc.vector.memset(eps[:], EPS)
        ident = resident.tile([P, P], F32, name="ident")
        make_identity(nc, ident[:])
        for s in range(len(slabs)):
            zero_plane(s, SLAB_BANKS if s == 0 else 1)

        x_sb = []
        for m in range(TOKEN_TILES):
            x_tile = resident.tile([P, D_MODEL], BF16, name="x%d" % m)
            x_sb.append(x_tile)
        for m in range(TOKEN_TILES):
            for half in range(2):
                columns = slice(half * D_MODEL // 2, (half + 1) * D_MODEL // 2)
                nc.sync.dma_start(out=x_sb[m][:, columns], in_=x_dram[:, m, columns])
            if m == 0:
                nc.sync.dma_start(out=gain_rows[0:1, 0:HEAD], in_=q_scale.unsqueeze(0))
                nc.sync.dma_start(out=gain_rows[0:1, HEAD : 2 * HEAD], in_=k_scale.unsqueeze(0))
        load_scales(0, 0)
        load_words(0, 0, 0, PASSES // 2)
        load_words(0, 0, PASSES // 2, PASSES // 2)
        cos_sb = resident.tile([P, TOKEN_TILES, HEAD], BF16, name="cos_sb")
        nc.sync.dma_start(out=cos_sb[:], in_=cos_dram)
        sin_sb = resident.tile([P, TOKEN_TILES, HEAD], BF16, name="sin_sb")
        nc.sync.dma_start(out=sin_sb[:], in_=sin_dram)
        load_scales(0, 1)
        load_words(0, 1, 0, PASSES)

        def load_slab(s):
            load_scales(s, 0)
            for b in range(SLAB_BANKS):
                load_words(s, b, 0, PASSES)

        load_slab(1)

        warm = resident.tile([P, 1], F32, name="warm")
        nc.scalar.activation(out=warm[:], in_=eps[:], func=ACT.Abs_reciprocal_sqrt)

        tables = [
            resident.tile([P, TOKEN_TILES, 2, HEAD], F32, name="table%d" % w) for w in range(2)
        ]
        gain_k = resident.tile([P, 2, HALF], F32, name="gain_k")
        turn_k = resident.tile([P, 2, HALF], F32, name="turn_k")

        def build_tables():
            gain_ps = psum.tile([P, BANK], F32, tag="bank", name="gain_ps")
            nc.tensor.matmul(
                out=gain_ps[:, 0 : 2 * HEAD], lhsT=ones[:], rhs=gain_rows[:], start=True, stop=True
            )
            spread_k = gain_ps[:, HEAD : 2 * HEAD].rearrange("p (a j) -> p a j", a=2)
            nc.scalar.copy(out=gain_k[:], in_=spread_k)
            nc.scalar.copy(out=turn_k[:, 0, :], in_=spread_k[:, 0, :])
            nc.scalar.mul(out=turn_k[:, 1, :], in_=spread_k[:, 1, :], mul=-1.0)

            nc.vector.tensor_tensor(
                out=tables[0][:, :, 0, :],
                in0=cos_sb[:],
                in1=gain_ps[:, 0:HEAD].unsqueeze(1).to_broadcast([P, TOKEN_TILES, HEAD]),
                op=ALU.mult,
            )
            nc.vector.tensor_tensor(
                out=tables[0][:, :, 1, 0:HALF],
                in0=sin_sb[:, :, HALF:HEAD],
                in1=gain_ps[:, 0:HALF].unsqueeze(1).to_broadcast([P, TOKEN_TILES, HALF]),
                op=ALU.mult,
            )
            nc.vector.scalar_tensor_tensor(
                out=tables[0][:, :, 1, HALF:HEAD],
                in0=sin_sb[:, :, 0:HALF],
                scalar=-1.0,
                in1=gain_ps[:, HALF:HEAD].unsqueeze(1).to_broadcast([P, TOKEN_TILES, HALF]),
                op0=ALU.mult,
                op1=ALU.mult,
            )

            shape = [P, TOKEN_TILES, 2, HALF]
            nc.gpsimd.tensor_tensor(
                out=tables[1][:, :, 0, :].rearrange("p m (a j) -> p m a j", a=2),
                in0=cos_sb[:].rearrange("p m (a j) -> p m a j", a=2),
                in1=gain_k[:].unsqueeze(1).to_broadcast(shape),
                op=ALU.mult,
            )
            nc.gpsimd.tensor_tensor(
                out=tables[1][:, :, 1, :].rearrange("p m (a j) -> p m a j", a=2),
                in0=sin_sb[:].rearrange("p m (a j) -> p m a j", a=2)[:, :, ::-1, :],
                in1=turn_k[:].unsqueeze(1).to_broadcast(shape),
                op=ALU.mult,
            )

        x_codes = []
        x_scales = []
        keep_warm(WARM_BEFORE)
        for m in range(TOKEN_TILES):
            x_pairs = x_sb[m][:].bitcast(F32)
            grouped = prep.tile([P, PASSES, P, PACK], BF16, align_bytes=64, name="grouped")
            grouped_pairs = grouped[:].bitcast(F32)
            for b in range(2):
                xt = psum.tile([P, 2, 2, P], F32, tag="bank", name="xt")
                for i in range(2):
                    g = 2 * b + i
                    for u in range(2):
                        nc.tensor.transpose(
                            out=xt[:, i, u, :],
                            in_=x_pairs[:, 256 * g + u : 256 * (g + 1) : 2],
                            identity=ident[:],
                        )
                nc.scalar.copy(
                    out=grouped_pairs[:, 2 * b : 2 * b + 2, :, :],
                    in_=xt[:].rearrange("p i u r -> p i r u"),
                )
                half_tile = 2 * m + b
                if half_tile % 3 > 0 and half_tile < WARM_UNTIL:
                    keep_warm(1)
            codes = resident.tile([P, CODES_SHIFT // 4 + PASSES * P], U32, align_bytes=256, name="x_codes%d" % m)
            scales = resident.tile([P, SCALES_SHIFT + PASSES * P], U8, align_bytes=256, name="x_scales%d" % m)
            nc.vector.quantize_mx(
                out=codes[:, CODES_SHIFT // 4 :].bitcast(FP8X4),
                scales=scales[:, SCALES_SHIFT:],
                in_=grouped[:].rearrange("p g r t -> p (g r t)"),
            )
            x_codes.append(codes[:, CODES_SHIFT // 4 :].rearrange("p (g r) -> p g r", g=PASSES))
            x_scales.append(scales[:, SCALES_SHIFT:].rearrange("p (g r) -> p g r", g=PASSES))
        build_tables()

        def project(s, m, b):
            columns = slice(BANK * b, BANK * (b + 1))
            planes = w_planes[s][0][:, :, columns] if len(w_planes[s]) == 1 else w_planes[s][b]
            acc = psum.tile([P, BANK], F32, tag="bank", name="acc")
            for g in range(PASSES):
                nc.tensor.matmul_mx(
                    out=acc[:],
                    lhsT=x_codes[m][:, g, :].bitcast(FP8X4),
                    lhsT_scale=x_scales[m][:, g, :],
                    rhs=w_words[s][b][:, g, :].bitcast(FP4X4),
                    rhs_scale=planes[:, g, :],
                    start=(g == 0),
                    stop=(g == PASSES - 1),
                )
            return acc

        def square_sums(acc):
            squared = squares.tile([P, BANK_HEADS, HEAD], F32, name="squared")
            sums = small.tile([P, BANK_HEADS], F32, name="sums")
            for h in range(BANK_HEADS):
                nc.scalar.activation(
                    out=squared[:, h, :],
                    in_=acc[:, h * HEAD : (h + 1) * HEAD],
                    func=ACT.Square,
                    accum_out=sums[:, h : h + 1],
                )
            return sums

        def norm_and_turn(s, m, b, acc, sums, shares):
            inv_rms = small.tile([P, BANK_HEADS], F32, name="inv_rms")
            nc.scalar.activation(
                out=inv_rms[:],
                in_=sums[:],
                func=ACT.Abs_reciprocal_sqrt,
                scale=1.0 / HEAD,
                bias=eps[:],
            )
            for h in range(BANK_HEADS):
                nc.vector.scalar_tensor_tensor(
                    out=shares[:, b * BANK_HEADS + h, :, :],
                    in0=acc[:, h * HEAD : (h + 1) * HEAD].unsqueeze(1).to_broadcast([P, 2, HEAD]),
                    scalar=inv_rms[:, h : h + 1],
                    in1=tables[slabs[s]["gain"]][:, m, :, :],
                    op0=ALU.mult,
                    op1=ALU.mult,
                )

        def add_and_store_bank(s, m, b, shares):
            slab = slabs[s]
            half = halves.tile([P, BANK_HEADS, HEAD], F32, name="half")
            heads = shares[:, b * BANK_HEADS : (b + 1) * BANK_HEADS]
            nc.gpsimd.tensor_tensor(
                out=half[:].rearrange("p h (a j) -> p h a j", a=2),
                in0=heads[:, :, 0, :].rearrange("p h (a j) -> p h a j", a=2),
                in1=heads[:, :, 1, :].rearrange("p h (a j) -> p h a j", a=2)[:, :, ::-1, :],
                op=ALU.add,
            )
            column = slab["first"] + b * BANK
            nc.sync.dma_start(
                out=slab["out"][:, m, column : column + BANK],
                in_=half[:].rearrange("p h j -> p (h j)"),
            )

        def add_and_store(s, m, shares):
            result = results.tile([P, SLAB_HEADS, HEAD], F32, name="result")
            add(nc.gpsimd, result, shares, 0, SLAB_HEADS)
            store_unit(s, m, result)

        def add(engine, result, shares, first, end):
            engine.tensor_tensor(
                out=result[:, first:end].rearrange("p h (a j) -> p h a j", a=2),
                in0=shares[:, first:end, 0, :].rearrange("p h (a j) -> p h a j", a=2),
                in1=shares[:, first:end, 1, :].rearrange("p h (a j) -> p h a j", a=2)[:, :, ::-1, :],
                op=ALU.add,
            )

        def store_unit(s, m, result):
            slab = slabs[s]
            nc.sync.dma_start(
                out=slab["out"][:, m, slab["first"] : slab["first"] + SLAB],
                in_=result[:].rearrange("p h j -> p (h j)"),
            )

        order = [(0, m, b) for b in range(SLAB_BANKS) for m in range(TOKEN_TILES)]
        order += [(s, m, b) for s in range(1, len(slabs)) for m in range(TOKEN_TILES) for b in range(SLAB_BANKS)]
        open_units = {}
        waiting = []
        half_done = []

        def finish_waiting():
            for s, m, b, acc, sums, shares in waiting:
                norm_and_turn(s, m, b, acc, sums, shares)
                units_left = (NORMED_SLABS - s) * TOKEN_TILES - m
                if s == 0:
                    add_and_store_bank(s, m, b, shares)
                elif units_left <= HELPED_UNITS:
                    if b == 0:
                        result = results.tile([P, SLAB_HEADS, HEAD], F32, name="result")
                        add(nc.gpsimd, result, shares, 0, BANK_HEADS)
                        half_done.append((s, m, result, shares))
                    elif units_left == 1:
                        for left_s, left_m, left_result, left_shares in half_done:
                            add(nc.vector, left_result, left_shares, BANK_HEADS, SLAB_HEADS)
                            store_unit(left_s, left_m, left_result)
                elif b == SLAB_BANKS - 1:
                    add_and_store(s, m, shares)
                if (s, m, b) in LOAD_BEHIND:
                    load_slab(LOAD_BEHIND[(s, m, b)])
            waiting.clear()

        for s, m, b in order:
            acc = project(s, m, b)
            if slabs[s]["gain"] is None:
                finish_waiting()
                if b == 0:
                    copied = copies.tile([P, SLAB], F32, name="copied")
                    open_units[(s, m)] = copied
                copied = open_units[(s, m)]
                if m < TOKEN_TILES - 1:
                    nc.scalar.copy(out=copied[:, b * BANK : (b + 1) * BANK], in_=acc[:])
                    if m == 0:
                        columns = slice(b * BANK, (b + 1) * BANK)
                        nc.scalar.dma_start(out=slabs[s]["out"][:, m, columns], in_=copied[:, columns])
                    elif b == SLAB_BANKS - 1:
                        nc.scalar.dma_start(out=slabs[s]["out"][:, m, :], in_=copied[:])
                else:
                    parts = 1 if b == 0 else 2
                    for part in range(parts):
                        first = b * BANK + part * BANK // parts
                        columns = slice(first, first + BANK // parts)
                        nc.scalar.copy(out=copied[:, columns], in_=acc[:, first - b * BANK : first - b * BANK + BANK // parts])
                        queue = nc.scalar if (b == SLAB_BANKS - 1 and part == parts - 1) else nc.sync
                        queue.dma_start(out=slabs[s]["out"][:, m, columns], in_=copied[:, columns])
            else:
                if b == 0:
                    shares = products.tile([P, SLAB_HEADS, 2, HEAD], F32, name="shares")
                    open_units[(s, m)] = shares
                shares = open_units[(s, m)]
                sums = square_sums(acc)
                finish_waiting()
                waiting.append((s, m, b, acc, sums, shares))
                if (s, m, b) == order[0]:
                    finish_waiting()
